import numpy as np
import ml_dtypes


def mxq(x, axis, fmt="e4m3"):
    dtype, down = {"e4m3": (ml_dtypes.float8_e4m3fn, 7), "e5m2": (ml_dtypes.float8_e5m2, 14)}[fmt]
    v = np.moveaxis(np.asarray(x, np.float32).astype(ml_dtypes.bfloat16).astype(np.float64), axis, -1)
    blocks = v.reshape(v.shape[:-1] + (-1, 32))
    amax = np.abs(blocks).max(-1, keepdims=True)
    byte = np.maximum(np.where(amax > 0, np.frexp(amax)[1] - 1 + 127, 0) - down, 1)
    scale = np.exp2(byte - 127.0)
    codes = (blocks / scale).astype(np.float32).astype(dtype).astype(np.float64)
    return np.moveaxis((codes * scale).reshape(v.shape), -1, axis)


WIDE = False


def mx_kscale(k):
    if not WIDE:
        return np.ones(k)
    levels = np.array([10, -10, 5, -5, 0])
    if k % 512:
        return np.exp2(np.random.permutation(np.resize(levels, k // 32))).repeat(32)
    a = np.empty((k // 512, 16))
    for p in range(k // 512):
        a[p, :8] = np.random.permutation(np.resize(levels, 8))
        for g in range(8):
            far = levels[np.abs(levels - a[p, g]) >= 10]
            a[p, g + 8] = far[np.random.randint(len(far))]
    return np.exp2(a.ravel()).repeat(32)


BF16 = ml_dtypes.bfloat16


def bf(x):
    return np.asarray(x, np.float32).astype(BF16)


def f64(x):
    return np.asarray(x).astype(np.float64)


B, P, WS, D, H = 4, 32, 8, 512, 8
HD = D // H
WN = P // WS
N = WS * WS
SHIFT = WS // 2
LN_EPS = 1e-5


def layer_norm(x, g, b):
    mu = x.mean(-1, keepdims=True)
    var = x.var(-1, keepdims=True)
    return (x - mu) / np.sqrt(var + LN_EPS) * g + b


def window_partition(img):
    x = img.reshape(B, WN, WS, WN, WS, D).transpose(0, 1, 3, 2, 4, 5)
    return x.reshape(B * WN * WN, N, D)


def heads(t):
    return t.reshape(B * WN * WN, N, H, HD).transpose(0, 2, 1, 3)


def setup_inputs():
    s = mx_kscale(D)
    x_mid = np.random.standard_normal((B, P * P, D)) * 1.4 + np.random.standard_normal((B, P * P, 1)) * 0.5
    return {"x_mid": bf(x_mid),
            "g3": bf((1.0 + 0.1 * np.random.standard_normal(D)) * s),
            "b3": bf(0.1 * np.random.standard_normal(D) * s),
            "Wqkv2": bf(np.random.standard_normal((D, 3 * D)) / np.sqrt(D) / s[:, None]),
            "bqkv2": bf(0.1 * np.random.standard_normal(3 * D))}


def reference(x_mid, g3, b3, Wqkv2, bqkv2):
    h = layer_norm(f64(x_mid), f64(g3), f64(b3))
    img = np.roll(h.reshape(B, P, P, D), (SHIFT, SHIFT), axis=(1, 2))
    w = window_partition(img)
    qkv = (mxq(w, 2, "e4m3") @ mxq(f64(Wqkv2), 0, "e4m3")) + f64(bqkv2)
    q, k, v = np.split(qkv, 3, axis=-1)
    return heads(q), heads(k), heads(v)

@@ -1,0 +1,242 @@
+from contextlib import ExitStack
+
+import concourse.mybir as mybir
+from concourse.masks import make_identity
+
+F32 = mybir.dt.float32
+BF16 = mybir.dt.bfloat16
+U8 = mybir.dt.uint8
+U32 = mybir.dt.uint32
+FP8X4 = mybir.dt.float8_e4m3fn_x4
+ACT = mybir.ActivationFunctionType
+ALU = mybir.AluOpType
+
+P = 128
+PACK = 4
+D = 512
+IMAGES = 4
+SIDE = 32
+WS = 8
+SHIFT = 4
+HEADS = 8
+HD = 64
+QUAD = 4
+QUADS = SIDE // QUAD
+UNIT_ROWS = P // QUADS
+UNIT_WINDOWS = 8
+UNITS = 2 * IMAGES
+TG = 2
+GROUP = TG * P
+LEAD = 2
+LN_EPS = 1e-5
+
+FLOPS = 2 * IMAGES * SIDE * SIDE * D * 3 * D
+
+
+def tile_successiveswintransfomerblock_pa_t_kernel(
+    tc, x_mid, g3, b3, Wqkv2, bqkv2, out_0, out_1, out_2
+):
+    nc = tc.nc
+    with ExitStack() as ctx:
+        const = ctx.enter_context(tc.tile_pool(name="const", bufs=1))
+        x_pool = ctx.enter_context(tc.tile_pool(name="x", bufs=UNITS))
+        stat_pool = ctx.enter_context(tc.tile_pool(name="stat", bufs=6))
+        junk_pool = ctx.enter_context(tc.tile_pool(name="junk", bufs=2))
+        xn_pool = ctx.enter_context(tc.tile_pool(name="xn", bufs=4))
+        h_pool = ctx.enter_context(tc.tile_pool(name="h", bufs=3))
+        q_pool = ctx.enter_context(tc.tile_pool(name="q", bufs=8))
+        o_pool = ctx.enter_context(tc.tile_pool(name="o", bufs=10))
+        psum_xt = ctx.enter_context(tc.psum_pool(name="psum_xt", bufs=2))
+        psum_acc = ctx.enter_context(tc.psum_pool(name="psum_acc", bufs=4))
+
+        def load_unit(u):
+            x_unit = x_pool.tile([P, QUAD, D], BF16)
+            quads = x_mid[u // 2].rearrange("(t jl) d -> t jl d", jl=QUAD)
+            first_row = (1 - u % 2) * UNIT_ROWS - SHIFT
+            if first_row < 0:
+                wrapped = -first_row * QUADS
+                nc.sync.dma_start(out=x_unit[0:wrapped], in_=quads[SIDE * QUADS - wrapped :])
+                nc.sync.dma_start(out=x_unit[wrapped:P], in_=quads[0 : P - wrapped])
+            else:
+                nc.sync.dma_start(
+                    out=x_unit[:], in_=quads[first_row * QUADS : first_row * QUADS + P]
+                )
+            return x_unit
+
+        x_units = [load_unit(0), load_unit(1)]
+
+        g_raw = const.tile([P, PACK], BF16)
+        b_raw = const.tile([P, PACK], BF16)
+        nc.sync.dma_start(out=g_raw[:], in_=g3.rearrange("(p c) -> p c", c=PACK))
+        nc.sync.dma_start(out=b_raw[:], in_=b3.rearrange("(p c) -> p c", c=PACK))
+
+        w_raw = const.tile([P, PACK, 3 * D], BF16)
+        nc.sync.dma_start(out=w_raw[:], in_=Wqkv2.rearrange("(p c) n -> p c n", c=PACK))
+
+        bias_bc = const.tile([P, 3 * D], BF16)
+        nc.sync.dma_start(out=bias_bc[:], in_=bqkv2.partition_broadcast(P))
+
+        for u in range(2, UNITS):
+            x_units.append(load_unit(u))
+
+        eps_col = const.tile([P, 1], F32)
+        nc.vector.memset(eps_col[:], LN_EPS)
+        warm = const.tile([P, 1], F32)
+        nc.scalar.activation(out=warm[:], in_=eps_col[:], func=ACT.Sqrt)
+
+        ident = const.tile([P, P], F32)
+        make_identity(nc, ident[:])
+
+        shifted = const.tile([P, P], F32)
+        ident_v = ident[:].rearrange("t (r q) -> t r q", q=QUADS)
+        shifted_v = shifted[:].rearrange("t (r q) -> t r q", q=QUADS)
+        nc.vector.tensor_copy(out=shifted_v[:, :, 1:QUADS], in_=ident_v[:, :, 0 : QUADS - 1])
+        nc.vector.tensor_copy(out=shifted_v[:, :, 0:1], in_=ident_v[:, :, QUADS - 1 : QUADS])
+        perm = const.tile([P, P], F32)
+        perm_v = perm[:].rearrange("t (i jh wr wc) -> t jh i wr wc", i=WS, jh=2, wr=2)
+        from_v = shifted[:].rearrange("t (wr i wc jh) -> t jh i wr wc", wr=2, i=WS, wc=4)
+        for jh in range(2):
+            nc.vector.tensor_copy(out=perm_v[:, jh], in_=from_v[:, jh])
+
+        gb_col = const.tile([P, 2 * PACK], F32)
+        nc.vector.tensor_copy(out=gb_col[:, 0:PACK], in_=g_raw[:])
+        nc.vector.tensor_copy(out=gb_col[:, PACK : 2 * PACK], in_=b_raw[:])
+
+        w_grouped = const.tile([P, 3 * D, PACK], BF16, align_bytes=64)
+        w_codes = const.tile([P, 3 * D], U32, align_bytes=64)
+        w_scales = const.tile([P, 3 * D], U8, align_bytes=64)
+
+        def prepare_weight(w):
+            cols = slice(w * D, (w + 1) * D)
+            by_column = w_raw[:, :, cols].rearrange("p c n -> p n c")
+            if w == 0:
+                nc.vector.tensor_copy(out=w_grouped[:, cols, :], in_=by_column)
+            else:
+                nc.scalar.copy(out=w_grouped[:, cols, :], in_=by_column)
+            nc.vector.quantize_mx(
+                out=w_codes[:, cols].bitcast(FP8X4),
+                scales=w_scales[:, cols],
+                in_=w_grouped[:, cols, :].rearrange("p n c -> p (n c)"),
+            )
+
+        def statistics_on_vector(x_grp):
+            parts = stat_pool.tile([P, TG, 6], F32)
+            mean_var = stat_pool.tile([P, TG, 2], F32)
+            for t in range(TG):
+                nc.vector.bn_stats(out=parts[:, t, :], in_=x_grp[:, t, :])
+            for t in range(TG):
+                nc.vector.bn_aggr(out=mean_var[:, t, :], in_=parts[:, t, :])
+            negmean = stat_pool.tile([P, TG], F32)
+            nc.vector.tensor_scalar_mul(out=negmean[:], in0=mean_var[:, :, 0], scalar1=-1.0)
+            return negmean, mean_var[:, :, 1], 1.0
+
+        def statistics_on_scalar(x_grp):
+            negmean = stat_pool.tile([P, TG], F32)
+            sumsq = stat_pool.tile([P, TG], F32)
+            junk_a = junk_pool.tile([P, TG, D], BF16)
+            junk_b = junk_pool.tile([P, TG, D], BF16)
+            for t in range(TG):
+                nc.scalar.activation(
+                    out=junk_a[:, t, :], in_=x_grp[:, t, :], func=ACT.Copy,
+                    scale=-1.0 / D, accum_out=negmean[:, t : t + 1],
+                )
+            for t in range(TG):
+                nc.scalar.activation(
+                    out=junk_b[:, t, :], in_=x_grp[:, t, :], func=ACT.Square,
+                    bias=negmean[:, t : t + 1], scale=1.0, accum_out=sumsq[:, t : t + 1],
+                )
+            return negmean, sumsq[:], 1.0 / D
+
+        def normalise_and_quantise(u, g):
+            x_grp = x_units[u][:, g * TG : (g + 1) * TG, :]
+            if u < 2:
+                negmean, spread, spread_scale = statistics_on_vector(x_grp)
+                regrouper = nc.vector
+            else:
+                negmean, spread, spread_scale = statistics_on_scalar(x_grp)
+                regrouper = nc.gpsimd
+            std = stat_pool.tile([P, TG], F32)
+            nc.scalar.activation(
+                out=std[:], in_=spread, func=ACT.Sqrt, scale=spread_scale, bias=eps_col[:, 0:1]
+            )
+            rstd = stat_pool.tile([P, TG], F32)
+            nc.vector.reciprocal(out=rstd[:], in_=std[:])
+
+            xn = xn_pool.tile([P, TG, PACK, P], F32)
+            for t in range(TG):
+                nc.gpsimd.tensor_scalar(
+                    out=xn[:, t, :, :], in0=x_grp[:, t, :].rearrange("m (p c) -> m c p", c=PACK),
+                    scalar1=negmean[:, t : t + 1], scalar2=rstd[:, t : t + 1],
+                    op0=ALU.add, op1=ALU.mult,
+                )
+
+            xt = [psum_xt.tile([P, 2, GROUP], F32, name="xt%d" % pair) for pair in range(2)]
+            for t in range(TG):
+                for c in range(PACK):
+                    nc.tensor.transpose(
+                        xt[c // 2][:, c % 2, t * P : (t + 1) * P],
+                        xn[:, t, c, :],
+                        perm[:],
+                    )
+
+            h_planes = h_pool.tile([P, PACK, GROUP], BF16)
+            for c in range(PACK):
+                nc.scalar.activation(
+                    out=h_planes[:, c, :], in_=xt[c // 2][:, c % 2, :], func=ACT.Identity,
+                    scale=gb_col[:, c : c + 1], bias=gb_col[:, PACK + c : PACK + c + 1],
+                )
+            h_grouped = h_pool.tile([P, GROUP, PACK], BF16, align_bytes=64)
+            regrouper.tensor_scalar(
+                out=h_grouped[:], in0=h_planes[:].rearrange("p c m -> p m c"),
+                scalar1=1.0, scalar2=0.0, op0=ALU.mult, op1=ALU.add,
+            )
+            h_codes = q_pool.tile([P, GROUP], U32, align_bytes=64)
+            h_scales = q_pool.tile([P, GROUP], U8, align_bytes=64)
+            nc.vector.quantize_mx(
+                out=h_codes[:].bitcast(FP8X4),
+                scales=h_scales[:],
+                in_=h_grouped[:].rearrange("p m c -> p (m c)"),
+            )
+            return h_codes, h_scales
+
+        def project_and_store(u, quantised):
+            first_window = (u // 2 * 2 + 1 - u % 2) * UNIT_WINDOWS
+            windows = slice(first_window, first_window + UNIT_WINDOWS)
+            for w, out_w in enumerate((out_0, out_1, out_2)):
+                cols = slice(w * D, (w + 1) * D)
+                o_tile = o_pool.tile([P, HEADS, QUAD, HD], F32)
+                for jl in range(QUAD):
+                    h_codes, h_scales = quantised[jl // TG]
+                    tokens = slice((jl % TG) * P, (jl % TG + 1) * P)
+                    acc = psum_acc.tile([P, D], F32)
+                    nc.tensor.matmul_mx(
+                        out=acc[:],
+                        lhsT=h_codes[:, tokens].bitcast(FP8X4),
+                        lhsT_scale=h_scales[:, tokens],
+                        rhs=w_codes[:, cols].bitcast(FP8X4),
+                        rhs_scale=w_scales[:, cols],
+                        start=True,
+                        stop=True,
+                    )
+                    nc.vector.tensor_tensor(
+                        out=o_tile[:, :, jl, :],
+                        in0=acc[:].rearrange("p (h f) -> p h f", h=HEADS),
+                        in1=bias_bc[:, cols].rearrange("p (h f) -> p h f", h=HEADS),
+                        op=ALU.add,
+                    )
+                nc.sync.dma_start(
+                    out=out_w[windows].rearrange("w h (x jl) f -> x (w h) (jl f)", jl=QUAD),
+                    in_=o_tile[:].rearrange("p h jl f -> p h (jl f)"),
+                )
+
+        def layer_norm_of_unit(u):
+            return [normalise_and_quantise(u, g) for g in range(QUAD // TG)]
+
+        prepare_weight(0)
+        quantised = [layer_norm_of_unit(u) for u in range(LEAD)]
+        prepare_weight(1)
+        prepare_weight(2)
+        for u in range(UNITS):
+            if u + LEAD < UNITS:
+                quantised.append(layer_norm_of_unit(u + LEAD))
+            project_and_store(u, quantised[u])

@@ -27,7 +27,8 @@ UNIT_WINDOWS = 8
 UNITS = 2 * IMAGES
 TG = 2
 GROUP = TG * P
-LEAD = 2
+GROUPS = 2 * UNITS
+HALF = P // 2
 LN_EPS = 1e-5
 
 FLOPS = 2 * IMAGES * SIDE * SIDE * D * 3 * D
@@ -37,206 +38,306 @@ def tile_successiveswintransfomerblock_pa_t_kernel(
     tc, x_mid, g3, b3, Wqkv2, bqkv2, out_0, out_1, out_2
 ):
     nc = tc.nc
+    outs = (out_0, out_1, out_2)
     with ExitStack() as ctx:
         const = ctx.enter_context(tc.tile_pool(name="const", bufs=1))
         x_pool = ctx.enter_context(tc.tile_pool(name="x", bufs=UNITS))
-        stat_pool = ctx.enter_context(tc.tile_pool(name="stat", bufs=6))
+        stat_pool = ctx.enter_context(tc.tile_pool(name="stat", bufs=8))
         junk_pool = ctx.enter_context(tc.tile_pool(name="junk", bufs=2))
         xn_pool = ctx.enter_context(tc.tile_pool(name="xn", bufs=4))
-        h_pool = ctx.enter_context(tc.tile_pool(name="h", bufs=3))
+        h_pool = ctx.enter_context(tc.tile_pool(name="h", bufs=4))
         q_pool = ctx.enter_context(tc.tile_pool(name="q", bufs=8))
-        o_pool = ctx.enter_context(tc.tile_pool(name="o", bufs=10))
+        o_pool = ctx.enter_context(tc.tile_pool(name="o", bufs=11))
         psum_xt = ctx.enter_context(tc.psum_pool(name="psum_xt", bufs=2))
         psum_acc = ctx.enter_context(tc.psum_pool(name="psum_acc", bufs=4))
+        ctx.enter_context(tc.manual_schedule())
 
-        def load_unit(u):
-            x_unit = x_pool.tile([P, QUAD, D], BF16)
+        def load_unit(u, jls=slice(0, QUAD)):
             quads = x_mid[u // 2].rearrange("(t jl) d -> t jl d", jl=QUAD)
             first_row = (1 - u % 2) * UNIT_ROWS - SHIFT
+            x_unit = x_units[u]
             if first_row < 0:
                 wrapped = -first_row * QUADS
                 nc.sync.dma_start(out=x_unit[0:wrapped], in_=quads[SIDE * QUADS - wrapped :])
                 nc.sync.dma_start(out=x_unit[wrapped:P], in_=quads[0 : P - wrapped])
             else:
                 nc.sync.dma_start(
-                    out=x_unit[:], in_=quads[first_row * QUADS : first_row * QUADS + P]
+                    out=x_unit[:, jls, :],
+                    in_=quads[first_row * QUADS : first_row * QUADS + P, jls, :],
                 )
-            return x_unit
 
-        x_units = [load_unit(0), load_unit(1)]
+        x_units = [x_pool.tile([P, QUAD, D], BF16, name="x_unit") for u in range(UNITS)]
+        load_unit(0, slice(0, TG))
+        load_unit(0, slice(TG, QUAD))
+        bias_row = const.tile([P, 3 * D], BF16)
+        nc.vector.memset(bias_row[:], 0.0)
+        nc.sync.dma_start(out=bias_row[0:1, :], in_=bqkv2.unsqueeze(0))
 
         g_raw = const.tile([P, PACK], BF16)
         b_raw = const.tile([P, PACK], BF16)
-        nc.sync.dma_start(out=g_raw[:], in_=g3.rearrange("(p c) -> p c", c=PACK))
-        nc.sync.dma_start(out=b_raw[:], in_=b3.rearrange("(p c) -> p c", c=PACK))
+        nc.scalar.dma_start(out=g_raw[:], in_=g3.rearrange("(p c) -> p c", c=PACK))
+        nc.scalar.dma_start(out=b_raw[:], in_=b3.rearrange("(p c) -> p c", c=PACK))
 
-        w_raw = const.tile([P, PACK, 3 * D], BF16)
-        nc.sync.dma_start(out=w_raw[:], in_=Wqkv2.rearrange("(p c) n -> p c n", c=PACK))
-
-        bias_bc = const.tile([P, 3 * D], BF16)
-        nc.sync.dma_start(out=bias_bc[:], in_=bqkv2.partition_broadcast(P))
-
+        w_rows = Wqkv2.rearrange("(p c) n -> p c n", c=PACK)
+        w_raw_q = const.tile([P, PACK, D], BF16)
+        w_raw_kv = const.tile([P, PACK, 2 * D], BF16)
+        nc.sync.dma_start(out=w_raw_q[:], in_=w_rows[:, :, 0:D])
+        load_unit(1)
+        nc.sync.dma_start(out=w_raw_kv[:], in_=w_rows[:, :, D : 3 * D])
+        w_raw = (w_raw_q[:], w_raw_kv[:, :, 0:D], w_raw_kv[:, :, D : 2 * D])
         for u in range(2, UNITS):
-            x_units.append(load_unit(u))
+            load_unit(u)
 
         eps_col = const.tile([P, 1], F32)
         nc.vector.memset(eps_col[:], LN_EPS)
         warm = const.tile([P, 1], F32)
-        nc.scalar.activation(out=warm[:], in_=eps_col[:], func=ACT.Sqrt)
+        nc.scalar.activation(out=warm[:], in_=eps_col[:], func=ACT.Abs_reciprocal_sqrt)
 
         ident = const.tile([P, P], F32)
         make_identity(nc, ident[:])
 
-        shifted = const.tile([P, P], F32)
-        ident_v = ident[:].rearrange("t (r q) -> t r q", q=QUADS)
-        shifted_v = shifted[:].rearrange("t (r q) -> t r q", q=QUADS)
-        nc.vector.tensor_copy(out=shifted_v[:, :, 1:QUADS], in_=ident_v[:, :, 0 : QUADS - 1])
-        nc.vector.tensor_copy(out=shifted_v[:, :, 0:1], in_=ident_v[:, :, QUADS - 1 : QUADS])
+        spread = const.tile([P, P], BF16)
+        nc.vector.memset(spread[:], 0.0)
+        nc.vector.memset(spread[0:1, :], 1.0)
+
         perm = const.tile([P, P], F32)
-        perm_v = perm[:].rearrange("t (i jh wr wc) -> t jh i wr wc", i=WS, jh=2, wr=2)
-        from_v = shifted[:].rearrange("t (wr i wc jh) -> t jh i wr wc", wr=2, i=WS, wc=4)
-        for jh in range(2):
-            nc.vector.tensor_copy(out=perm_v[:, jh], in_=from_v[:, jh])
+        perm_v = perm[:].rearrange("t (r jh wc) -> t r jh wc", jh=2, wc=4)
+        ident_v = ident[:].rearrange("t (r q e) -> t r q e", q=4, e=2)
+        nc.vector.tensor_copy(out=perm_v[:, :, 1, :], in_=ident_v[:, :, :, 0])
+        nc.vector.tensor_copy(out=perm_v[:, :, 0, 1:4], in_=ident_v[:, :, 0:3, 1])
+        nc.vector.tensor_copy(out=perm_v[:, :, 0, 0:1], in_=ident_v[:, :, 3:4, 1])
 
         gb_col = const.tile([P, 2 * PACK], F32)
-        nc.vector.tensor_copy(out=gb_col[:, 0:PACK], in_=g_raw[:])
-        nc.vector.tensor_copy(out=gb_col[:, PACK : 2 * PACK], in_=b_raw[:])
+
+        def widen_gain_and_bias():
+            nc.vector.tensor_copy(out=gb_col[:, 0:PACK], in_=g_raw[:])
+            nc.vector.tensor_copy(out=gb_col[:, PACK : 2 * PACK], in_=b_raw[:])
+
+        bias_bc = const.tile([P, 3 * D], BF16)
+
+        def spread_bias(w):
+            cols = slice(w * D, (w + 1) * D)
+            bias_ps = psum_acc.tile([P, D], F32, name="acc")
+            nc.tensor.matmul(bias_ps[:], lhsT=spread[:], rhs=bias_row[:, cols], start=True, stop=True)
+            nc.scalar.copy(out=bias_bc[:, cols], in_=bias_ps[:])
 
         w_grouped = const.tile([P, 3 * D, PACK], BF16, align_bytes=64)
         w_codes = const.tile([P, 3 * D], U32, align_bytes=64)
         w_scales = const.tile([P, 3 * D], U8, align_bytes=64)
 
-        def prepare_weight(w):
+        def regroup_weight(w):
             cols = slice(w * D, (w + 1) * D)
-            by_column = w_raw[:, :, cols].rearrange("p c n -> p n c")
             if w == 0:
-                nc.vector.tensor_copy(out=w_grouped[:, cols, :], in_=by_column)
+                nc.vector.tensor_copy(
+                    out=w_grouped[:, cols, :], in_=w_raw[w].rearrange("p c n -> p n c")
+                )
             else:
-                nc.scalar.copy(out=w_grouped[:, cols, :], in_=by_column)
+                nc.gpsimd.tensor_scalar(
+                    out=w_grouped[:, cols, :], in0=w_raw[w].rearrange("p c n -> p n c"),
+                    scalar1=1.0, scalar2=0.0, op0=ALU.mult, op1=ALU.add,
+                )
+
+        def quantise_weight(w):
+            cols = slice(w * D, (w + 1) * D)
             nc.vector.quantize_mx(
                 out=w_codes[:, cols].bitcast(FP8X4),
                 scales=w_scales[:, cols],
                 in_=w_grouped[:, cols, :].rearrange("p n c -> p (n c)"),
             )
 
-        def statistics_on_vector(x_grp):
+        stats = {}
+        normal = {}
+        planes = {}
+        grouped = {}
+        codes = {}
+        banks = {}
+
+        def x_of(gr):
+            return x_units[gr // 2][:, (gr % 2) * TG : (gr % 2 + 1) * TG, :]
+
+        def reciprocal_std(gr, negmean, spread_of, scale):
+            rstd = stat_pool.tile([P, TG], F32)
+            nc.scalar.activation(
+                out=rstd[:], in_=spread_of, func=ACT.Abs_reciprocal_sqrt,
+                scale=scale, bias=eps_col[:, 0:1],
+            )
+            stats[gr] = (negmean, rstd)
+
+        def statistics_on_vector(gr):
             parts = stat_pool.tile([P, TG, 6], F32)
             mean_var = stat_pool.tile([P, TG, 2], F32)
             for t in range(TG):
-                nc.vector.bn_stats(out=parts[:, t, :], in_=x_grp[:, t, :])
+                nc.vector.bn_stats(out=parts[:, t, :], in_=x_of(gr)[:, t, :])
             for t in range(TG):
                 nc.vector.bn_aggr(out=mean_var[:, t, :], in_=parts[:, t, :])
             negmean = stat_pool.tile([P, TG], F32)
             nc.vector.tensor_scalar_mul(out=negmean[:], in0=mean_var[:, :, 0], scalar1=-1.0)
-            return negmean, mean_var[:, :, 1], 1.0
+            reciprocal_std(gr, negmean, mean_var[:, :, 1], 1.0)
 
-        def statistics_on_scalar(x_grp):
+        def statistics_on_scalar(gr):
             negmean = stat_pool.tile([P, TG], F32)
             sumsq = stat_pool.tile([P, TG], F32)
             junk_a = junk_pool.tile([P, TG, D], BF16)
             junk_b = junk_pool.tile([P, TG, D], BF16)
             for t in range(TG):
                 nc.scalar.activation(
-                    out=junk_a[:, t, :], in_=x_grp[:, t, :], func=ACT.Copy,
+                    out=junk_a[:, t, :], in_=x_of(gr)[:, t, :], func=ACT.Copy,
                     scale=-1.0 / D, accum_out=negmean[:, t : t + 1],
                 )
             for t in range(TG):
                 nc.scalar.activation(
-                    out=junk_b[:, t, :], in_=x_grp[:, t, :], func=ACT.Square,
+                    out=junk_b[:, t, :], in_=x_of(gr)[:, t, :], func=ACT.Square,
                     bias=negmean[:, t : t + 1], scale=1.0, accum_out=sumsq[:, t : t + 1],
                 )
-            return negmean, sumsq[:], 1.0 / D
+            reciprocal_std(gr, negmean, sumsq[:], 1.0 / D)
 
-        def normalise_and_quantise(u, g):
-            x_grp = x_units[u][:, g * TG : (g + 1) * TG, :]
-            if u < 2:
-                negmean, spread, spread_scale = statistics_on_vector(x_grp)
-                regrouper = nc.vector
-            else:
-                negmean, spread, spread_scale = statistics_on_scalar(x_grp)
-                regrouper = nc.gpsimd
-            std = stat_pool.tile([P, TG], F32)
-            nc.scalar.activation(
-                out=std[:], in_=spread, func=ACT.Sqrt, scale=spread_scale, bias=eps_col[:, 0:1]
-            )
-            rstd = stat_pool.tile([P, TG], F32)
-            nc.vector.reciprocal(out=rstd[:], in_=std[:])
-
+        def normalise(gr, help_of_scalar=False):
+            negmean, rstd = stats[gr]
             xn = xn_pool.tile([P, TG, PACK, P], F32)
-            for t in range(TG):
-                nc.gpsimd.tensor_scalar(
-                    out=xn[:, t, :, :], in0=x_grp[:, t, :].rearrange("m (p c) -> m c p", c=PACK),
-                    scalar1=negmean[:, t : t + 1], scalar2=rstd[:, t : t + 1],
-                    op0=ALU.add, op1=ALU.mult,
-                )
+            for t in reversed(range(TG)):
+                x_t = x_of(gr)[:, t, :].rearrange("m (p c) -> m c p", c=PACK)
+                if help_of_scalar and t == 1:
+                    shift = stat_pool.tile([P, 1], F32)
+                    nc.gpsimd.tensor_tensor(
+                        out=shift[:], in0=negmean[:, t : t + 1], in1=rstd[:, t : t + 1],
+                        op=ALU.mult,
+                    )
+                    nc.scalar.activation(
+                        out=xn[:, t, :, :], in_=x_t, func=ACT.Identity,
+                        scale=rstd[:, t : t + 1], bias=shift[:, 0:1],
+                    )
+                else:
+                    nc.gpsimd.tensor_scalar(
+                        out=xn[:, t, :, :], in0=x_t,
+                        scalar1=negmean[:, t : t + 1], scalar2=rstd[:, t : t + 1],
+                        op0=ALU.add, op1=ALU.mult,
+                    )
+            normal[gr] = xn
 
+        def transpose(gr):
             xt = [psum_xt.tile([P, 2, GROUP], F32, name="xt%d" % pair) for pair in range(2)]
             for t in range(TG):
                 for c in range(PACK):
                     nc.tensor.transpose(
-                        xt[c // 2][:, c % 2, t * P : (t + 1) * P],
-                        xn[:, t, c, :],
-                        perm[:],
+                        xt[c // 2][:, c % 2, t * P : (t + 1) * P], normal[gr][:, t, c, :], perm[:]
                     )
+            banks[gr] = xt
 
+        def gain_and_bias(gr):
             h_planes = h_pool.tile([P, PACK, GROUP], BF16)
             for c in range(PACK):
                 nc.scalar.activation(
-                    out=h_planes[:, c, :], in_=xt[c // 2][:, c % 2, :], func=ACT.Identity,
+                    out=h_planes[:, c, :], in_=banks[gr][c // 2][:, c % 2, :], func=ACT.Identity,
                     scale=gb_col[:, c : c + 1], bias=gb_col[:, PACK + c : PACK + c + 1],
                 )
+            planes[gr] = h_planes
+
+        def regroup(gr, engine):
             h_grouped = h_pool.tile([P, GROUP, PACK], BF16, align_bytes=64)
-            regrouper.tensor_scalar(
-                out=h_grouped[:], in0=h_planes[:].rearrange("p c m -> p m c"),
+            engine.tensor_scalar(
+                out=h_grouped[:], in0=planes[gr][:].rearrange("p c m -> p m c"),
                 scalar1=1.0, scalar2=0.0, op0=ALU.mult, op1=ALU.add,
             )
+            grouped[gr] = h_grouped
+
+        def quantise(gr):
             h_codes = q_pool.tile([P, GROUP], U32, align_bytes=64)
             h_scales = q_pool.tile([P, GROUP], U8, align_bytes=64)
             nc.vector.quantize_mx(
                 out=h_codes[:].bitcast(FP8X4),
                 scales=h_scales[:],
-                in_=h_grouped[:].rearrange("p m c -> p (m c)"),
+                in_=grouped[gr][:].rearrange("p m c -> p (m c)"),
             )
-            return h_codes, h_scales
+            codes[gr] = (h_codes, h_scales)
 
-        def project_and_store(u, quantised):
-            first_window = (u // 2 * 2 + 1 - u % 2) * UNIT_WINDOWS
-            windows = slice(first_window, first_window + UNIT_WINDOWS)
-            for w, out_w in enumerate((out_0, out_1, out_2)):
-                cols = slice(w * D, (w + 1) * D)
-                o_tile = o_pool.tile([P, HEADS, QUAD, HD], F32)
-                for jl in range(QUAD):
-                    h_codes, h_scales = quantised[jl // TG]
-                    tokens = slice((jl % TG) * P, (jl % TG + 1) * P)
-                    acc = psum_acc.tile([P, D], F32)
-                    nc.tensor.matmul_mx(
-                        out=acc[:],
-                        lhsT=h_codes[:, tokens].bitcast(FP8X4),
-                        lhsT_scale=h_scales[:, tokens],
-                        rhs=w_codes[:, cols].bitcast(FP8X4),
-                        rhs_scale=w_scales[:, cols],
-                        start=True,
-                        stop=True,
-                    )
-                    nc.vector.tensor_tensor(
-                        out=o_tile[:, :, jl, :],
-                        in0=acc[:].rearrange("p (h f) -> p h f", h=HEADS),
-                        in1=bias_bc[:, cols].rearrange("p (h f) -> p h f", h=HEADS),
-                        op=ALU.add,
-                    )
-                nc.sync.dma_start(
-                    out=out_w[windows].rearrange("w h (x jl) f -> x (w h) (jl f)", jl=QUAD),
-                    in_=o_tile[:].rearrange("p h jl f -> p h (jl f)"),
-                )
+        o_tiles = {}
 
-        def layer_norm_of_unit(u):
-            return [normalise_and_quantise(u, g) for g in range(QUAD // TG)]
+        def project(u, w, jl):
+            cols = slice(w * D, (w + 1) * D)
+            if jl == 0:
+                o_tiles[u, w] = o_pool.tile([P, HEADS, QUAD, HD], F32, name="o_tile")
+            h_codes, h_scales = codes[2 * u + jl // TG]
+            tokens = slice((jl % TG) * P, (jl % TG + 1) * P)
+            acc = psum_acc.tile([P, D], F32)
+            nc.tensor.matmul_mx(
+                out=acc[:],
+                lhsT=h_codes[:, tokens].bitcast(FP8X4),
+                lhsT_scale=h_scales[:, tokens],
+                rhs=w_codes[:, cols].bitcast(FP8X4),
+                rhs_scale=w_scales[:, cols],
+                start=True,
+                stop=True,
+            )
+            nc.vector.tensor_tensor(
+                out=o_tiles[u, w][:, :, jl, :],
+                in0=acc[:].rearrange("p (h f) -> p h f", h=HEADS),
+                in1=bias_bc[:, cols].rearrange("p (h f) -> p h f", h=HEADS),
+                op=ALU.add,
+            )
 
-        prepare_weight(0)
-        quantised = [layer_norm_of_unit(u) for u in range(LEAD)]
-        prepare_weight(1)
-        prepare_weight(2)
-        for u in range(UNITS):
-            if u + LEAD < UNITS:
-                quantised.append(layer_norm_of_unit(u + LEAD))
-            project_and_store(u, quantised[u])
+        def store(u, w, wr, queue):
+            first_window = (u // 2 * 2 + 1 - u % 2) * UNIT_WINDOWS + wr * 4
+            queue.dma_start(
+                out=outs[w][first_window : first_window + 4].rearrange(
+                    "w h (x jl) f -> x (w h) (jl f)", jl=QUAD
+                ),
+                in_=o_tiles[u, w][wr * HALF : (wr + 1) * HALF].rearrange("p h jl f -> p h (jl f)"),
+            )
+
+        def statistics(gr):
+            if gr < 3 or gr == GROUPS // 2:
+                statistics_on_vector(gr)
+            else:
+                statistics_on_scalar(gr)
+
+        statistics(0)
+        normalise(0, help_of_scalar=True)
+        statistics(1)
+        widen_gain_and_bias()
+        transpose(0)
+        normalise(1, help_of_scalar=True)
+        regroup_weight(0)
+        quantise_weight(0)
+        gain_and_bias(0)
+        spread_bias(0)
+        regroup(0, nc.vector)
+        quantise(0)
+        transpose(1)
+        gain_and_bias(1)
+        statistics(2)
+        normalise(2)
+        regroup_weight(1)
+        regroup_weight(2)
+        for w in range(1, 3):
+            spread_bias(w)
+        statistics(3)
+
+        waiting = []
+        for s in range(GROUPS):
+            u = s // 2
+            turns = [(w, jl) for w in range(3) for jl in range(QUAD)][(s % 2) * 6 : (s % 2) * 6 + 6]
+            transpose_at = 5 if s == 0 else 1
+            quantise_at = 2 if s == 0 else (1, 5)[s % 2]
+            if s + 3 < GROUPS:
+                normalise(s + 3)
+            for n, (w, jl) in enumerate(turns):
+                if n == quantise_at and s + 1 < GROUPS:
+                    if s == 0:
+                        regroup(1, nc.vector)
+                    quantise(s + 1)
+                if u == 0 and w > 0 and jl == 0:
+                    quantise_weight(w)
+                project(u, w, jl)
+                if n == transpose_at and s + 2 < GROUPS:
+                    transpose(s + 2)
+                    gain_and_bias(s + 2)
+                    regroup(s + 2, nc.gpsimd)
+                if jl == QUAD - 1:
+                    store(u, w, 0, nc.sync)
+                    for late in waiting:
+                        store(*late, 1, nc.scalar)
+                    waiting = [(u, w)]
+            if s + 4 < GROUPS:
+                statistics(s + 4)
+        for late in waiting:
+            store(*late, 1, nc.scalar)

@@ -28,7 +28,6 @@ UNITS = 2 * IMAGES
 TG = 2
 GROUP = TG * P
 GROUPS = 2 * UNITS
-HALF = P // 2
 LN_EPS = 1e-5
 
 FLOPS = 2 * IMAGES * SIDE * SIDE * D * 3 * D
@@ -101,11 +100,12 @@ def tile_successiveswintransfomerblock_pa_t_kernel(
         nc.vector.memset(spread[0:1, :], 1.0)
 
         perm = const.tile([P, P], F32)
-        perm_v = perm[:].rearrange("t (r jh wc) -> t r jh wc", jh=2, wc=4)
-        ident_v = ident[:].rearrange("t (r q e) -> t r q e", q=4, e=2)
-        nc.vector.tensor_copy(out=perm_v[:, :, 1, :], in_=ident_v[:, :, :, 0])
-        nc.vector.tensor_copy(out=perm_v[:, :, 0, 1:4], in_=ident_v[:, :, 0:3, 1])
-        nc.vector.tensor_copy(out=perm_v[:, :, 0, 0:1], in_=ident_v[:, :, 3:4, 1])
+        perm_v = perm[:].rearrange("t (i jh wr wc) -> t jh wr i wc", i=WS, jh=2, wr=2)
+        ident_v = ident[:].rearrange("t (wr i q e) -> t e wr i q", wr=2, i=WS, e=2)
+        for wr in range(2):
+            nc.vector.tensor_copy(out=perm_v[:, 1, wr], in_=ident_v[:, 0, wr])
+            nc.vector.tensor_copy(out=perm_v[:, 0, wr, :, 1:4], in_=ident_v[:, 1, wr, :, 0:3])
+            nc.vector.tensor_copy(out=perm_v[:, 0, wr, :, 0:1], in_=ident_v[:, 1, wr, :, 3:4])
 
         gb_col = const.tile([P, 2 * PACK], F32)
 
@@ -275,17 +275,17 @@ def tile_successiveswintransfomerblock_pa_t_kernel(
                 op=ALU.add,
             )
 
-        def store(u, w, wr, queue):
-            first_window = (u // 2 * 2 + 1 - u % 2) * UNIT_WINDOWS + wr * 4
-            queue.dma_start(
-                out=outs[w][first_window : first_window + 4].rearrange(
+        def store(u, w):
+            first_window = (u // 2 * 2 + 1 - u % 2) * UNIT_WINDOWS
+            nc.sync.dma_start(
+                out=outs[w][first_window : first_window + UNIT_WINDOWS].rearrange(
                     "w h (x jl) f -> x (w h) (jl f)", jl=QUAD
                 ),
-                in_=o_tiles[u, w][wr * HALF : (wr + 1) * HALF].rearrange("p h jl f -> p h (jl f)"),
+                in_=o_tiles[u, w][:].rearrange("p h jl f -> p h (jl f)"),
             )
 
         def statistics(gr):
-            if gr < 3 or gr == GROUPS // 2:
+            if gr < 3:
                 statistics_on_vector(gr)
             else:
                 statistics_on_scalar(gr)
@@ -305,19 +305,18 @@ def tile_successiveswintransfomerblock_pa_t_kernel(
         transpose(1)
         gain_and_bias(1)
         statistics(2)
-        normalise(2)
         regroup_weight(1)
+        normalise(2)
         regroup_weight(2)
         for w in range(1, 3):
             spread_bias(w)
         statistics(3)
 
-        waiting = []
         for s in range(GROUPS):
             u = s // 2
             turns = [(w, jl) for w in range(3) for jl in range(QUAD)][(s % 2) * 6 : (s % 2) * 6 + 6]
             transpose_at = 5 if s == 0 else 1
-            quantise_at = 2 if s == 0 else (1, 5)[s % 2]
+            quantise_at = 2 if s == 0 else (1, 4)[s % 2]
             if s + 3 < GROUPS:
                 normalise(s + 3)
             for n, (w, jl) in enumerate(turns):
@@ -333,11 +332,6 @@ def tile_successiveswintransfomerblock_pa_t_kernel(
                     gain_and_bias(s + 2)
                     regroup(s + 2, nc.gpsimd)
                 if jl == QUAD - 1:
-                    store(u, w, 0, nc.sync)
-                    for late in waiting:
-                        store(*late, 1, nc.scalar)
-                    waiting = [(u, w)]
+                    store(u, w)
             if s + 4 < GROUPS:
                 statistics(s + 4)
-        for late in waiting:
-            store(*late, 1, nc.scalar)

@@ -81,10 +81,9 @@ def tile_successiveswintransfomerblock_pa_t_kernel(
         w_raw_q = const.tile([P, PACK, D], BF16)
         w_raw_kv = const.tile([P, PACK, 2 * D], BF16)
         nc.sync.dma_start(out=w_raw_q[:], in_=w_rows[:, :, 0:D])
-        load_unit(1)
         nc.sync.dma_start(out=w_raw_kv[:], in_=w_rows[:, :, D : 3 * D])
         w_raw = (w_raw_q[:], w_raw_kv[:, :, 0:D], w_raw_kv[:, :, D : 2 * D])
-        for u in range(2, UNITS):
+        for u in range(1, UNITS):
             load_unit(u)
 
         eps_col = const.tile([P, 1], F32)
@@ -285,7 +284,7 @@ def tile_successiveswintransfomerblock_pa_t_kernel(
             )
 
         def statistics(gr):
-            if gr < 3:
+            if gr < 2:
                 statistics_on_vector(gr)
             else:
                 statistics_on_scalar(gr)
@@ -303,29 +302,29 @@ def tile_successiveswintransfomerblock_pa_t_kernel(
         regroup(0, nc.vector)
         quantise(0)
         transpose(1)
-        gain_and_bias(1)
-        statistics(2)
         regroup_weight(1)
-        normalise(2)
+        gain_and_bias(1)
+        regroup(1, nc.vector)
+        quantise(1)
+        spread_bias(1)
+        statistics(2)
         regroup_weight(2)
-        for w in range(1, 3):
-            spread_bias(w)
+        spread_bias(2)
         statistics(3)
+        normalise(2)
 
         for s in range(GROUPS):
             u = s // 2
             turns = [(w, jl) for w in range(3) for jl in range(QUAD)][(s % 2) * 6 : (s % 2) * 6 + 6]
-            transpose_at = 5 if s == 0 else 1
-            quantise_at = 2 if s == 0 else (1, 4)[s % 2]
+            transpose_at = (5, 2)[s] if s < 2 else 1
+            quantise_at = (1, 4)[s % 2]
             if s + 3 < GROUPS:
                 normalise(s + 3)
             for n, (w, jl) in enumerate(turns):
-                if n == quantise_at and s + 1 < GROUPS:
-                    if s == 0:
-                        regroup(1, nc.vector)
+                if n == quantise_at and 0 < s < GROUPS - 1:
                     quantise(s + 1)
-                if u == 0 and w > 0 and jl == 0:
-                    quantise_weight(w)
+                if u == 0 and w < 2 and jl == 2:
+                    quantise_weight(w + 1)
                 project(u, w, jl)
                 if n == transpose_at and s + 2 < GROUPS:
                     transpose(s + 2)

from contextlib import ExitStack

import concourse.mybir as mybir
from concourse.masks import make_identity

F32 = mybir.dt.float32
BF16 = mybir.dt.bfloat16
U8 = mybir.dt.uint8
U32 = mybir.dt.uint32
FP8X4 = mybir.dt.float8_e4m3fn_x4
ACT = mybir.ActivationFunctionType
ALU = mybir.AluOpType

P = 128
PACK = 4
D = 512
IMAGES = 4
SIDE = 32
WS = 8
SHIFT = 4
HEADS = 8
HD = 64
QUAD = 4
QUADS = SIDE // QUAD
UNIT_ROWS = P // QUADS
UNIT_WINDOWS = 8
UNITS = 2 * IMAGES
TG = 2
GROUP = TG * P
GROUPS = 2 * UNITS
LN_EPS = 1e-5

FLOPS = 2 * IMAGES * SIDE * SIDE * D * 3 * D


def tile_successiveswintransfomerblock_pa_t_kernel(
    tc, x_mid, g3, b3, Wqkv2, bqkv2, out_0, out_1, out_2
):
    nc = tc.nc
    outs = (out_0, out_1, out_2)
    with ExitStack() as ctx:
        const = ctx.enter_context(tc.tile_pool(name="const", bufs=1))
        x_pool = ctx.enter_context(tc.tile_pool(name="x", bufs=UNITS))
        stat_pool = ctx.enter_context(tc.tile_pool(name="stat", bufs=8))
        junk_pool = ctx.enter_context(tc.tile_pool(name="junk", bufs=2))
        xn_pool = ctx.enter_context(tc.tile_pool(name="xn", bufs=4))
        h_pool = ctx.enter_context(tc.tile_pool(name="h", bufs=4))
        q_pool = ctx.enter_context(tc.tile_pool(name="q", bufs=8))
        o_pool = ctx.enter_context(tc.tile_pool(name="o", bufs=11))
        psum_xt = ctx.enter_context(tc.psum_pool(name="psum_xt", bufs=2))
        psum_acc = ctx.enter_context(tc.psum_pool(name="psum_acc", bufs=4))
        ctx.enter_context(tc.manual_schedule())

        def load_unit(u, jls=slice(0, QUAD)):
            quads = x_mid[u // 2].rearrange("(t jl) d -> t jl d", jl=QUAD)
            first_row = (1 - u % 2) * UNIT_ROWS - SHIFT
            x_unit = x_units[u]
            if first_row < 0:
                wrapped = -first_row * QUADS
                nc.sync.dma_start(out=x_unit[0:wrapped], in_=quads[SIDE * QUADS - wrapped :])
                nc.sync.dma_start(out=x_unit[wrapped:P], in_=quads[0 : P - wrapped])
            else:
                nc.sync.dma_start(
                    out=x_unit[:, jls, :],
                    in_=quads[first_row * QUADS : first_row * QUADS + P, jls, :],
                )

        x_units = [x_pool.tile([P, QUAD, D], BF16, name="x_unit") for u in range(UNITS)]
        load_unit(0, slice(0, TG))
        load_unit(0, slice(TG, QUAD))
        bias_row = const.tile([P, 3 * D], BF16)
        nc.vector.memset(bias_row[:], 0.0)
        nc.sync.dma_start(out=bias_row[0:1, :], in_=bqkv2.unsqueeze(0))

        g_raw = const.tile([P, PACK], BF16)
        b_raw = const.tile([P, PACK], BF16)
        nc.scalar.dma_start(out=g_raw[:], in_=g3.rearrange("(p c) -> p c", c=PACK))
        nc.scalar.dma_start(out=b_raw[:], in_=b3.rearrange("(p c) -> p c", c=PACK))

        w_rows = Wqkv2.rearrange("(p c) n -> p c n", c=PACK)
        w_raw_q = const.tile([P, PACK, D], BF16)
        w_raw_kv = const.tile([P, PACK, 2 * D], BF16)
        nc.sync.dma_start(out=w_raw_q[:], in_=w_rows[:, :, 0:D])
        nc.sync.dma_start(out=w_raw_kv[:], in_=w_rows[:, :, D : 3 * D])
        w_raw = (w_raw_q[:], w_raw_kv[:, :, 0:D], w_raw_kv[:, :, D : 2 * D])
        for u in range(1, UNITS):
            load_unit(u)

        eps_col = const.tile([P, 1], F32)
        nc.vector.memset(eps_col[:], LN_EPS)
        warm = const.tile([P, 1], F32)
        nc.scalar.activation(out=warm[:], in_=eps_col[:], func=ACT.Abs_reciprocal_sqrt)

        ident = const.tile([P, P], F32)
        make_identity(nc, ident[:])

        spread = const.tile([P, P], BF16)
        nc.vector.memset(spread[:], 0.0)
        nc.vector.memset(spread[0:1, :], 1.0)

        perm = const.tile([P, P], F32)
        perm_v = perm[:].rearrange("t (i jh wr wc) -> t jh wr i wc", i=WS, jh=2, wr=2)
        ident_v = ident[:].rearrange("t (wr i q e) -> t e wr i q", wr=2, i=WS, e=2)
        for wr in range(2):
            nc.vector.tensor_copy(out=perm_v[:, 1, wr], in_=ident_v[:, 0, wr])
            nc.vector.tensor_copy(out=perm_v[:, 0, wr, :, 1:4], in_=ident_v[:, 1, wr, :, 0:3])
            nc.vector.tensor_copy(out=perm_v[:, 0, wr, :, 0:1], in_=ident_v[:, 1, wr, :, 3:4])

        gb_col = const.tile([P, 2 * PACK], F32)

        def widen_gain_and_bias():
            nc.vector.tensor_copy(out=gb_col[:, 0:PACK], in_=g_raw[:])
            nc.vector.tensor_copy(out=gb_col[:, PACK : 2 * PACK], in_=b_raw[:])

        bias_bc = const.tile([P, 3 * D], BF16)

        def spread_bias(w):
            cols = slice(w * D, (w + 1) * D)
            bias_ps = psum_acc.tile([P, D], F32, name="acc")
            nc.tensor.matmul(bias_ps[:], lhsT=spread[:], rhs=bias_row[:, cols], start=True, stop=True)
            nc.scalar.copy(out=bias_bc[:, cols], in_=bias_ps[:])

        w_grouped = const.tile([P, 3 * D, PACK], BF16, align_bytes=64)
        w_codes = const.tile([P, 3 * D], U32, align_bytes=64)
        w_scales = const.tile([P, 3 * D], U8, align_bytes=64)

        def regroup_weight(w):
            cols = slice(w * D, (w + 1) * D)
            if w == 0:
                nc.vector.tensor_copy(
                    out=w_grouped[:, cols, :], in_=w_raw[w].rearrange("p c n -> p n c")
                )
            else:
                nc.gpsimd.tensor_scalar(
                    out=w_grouped[:, cols, :], in0=w_raw[w].rearrange("p c n -> p n c"),
                    scalar1=1.0, scalar2=0.0, op0=ALU.mult, op1=ALU.add,
                )

        def quantise_weight(w):
            cols = slice(w * D, (w + 1) * D)
            nc.vector.quantize_mx(
                out=w_codes[:, cols].bitcast(FP8X4),
                scales=w_scales[:, cols],
                in_=w_grouped[:, cols, :].rearrange("p n c -> p (n c)"),
            )

        stats = {}
        normal = {}
        planes = {}
        grouped = {}
        codes = {}
        banks = {}

        def x_of(gr):
            return x_units[gr // 2][:, (gr % 2) * TG : (gr % 2 + 1) * TG, :]

        def reciprocal_std(gr, negmean, spread_of, scale):
            rstd = stat_pool.tile([P, TG], F32)
            nc.scalar.activation(
                out=rstd[:], in_=spread_of, func=ACT.Abs_reciprocal_sqrt,
                scale=scale, bias=eps_col[:, 0:1],
            )
            stats[gr] = (negmean, rstd)

        def statistics_on_vector(gr):
            parts = stat_pool.tile([P, TG, 6], F32)
            mean_var = stat_pool.tile([P, TG, 2], F32)
            for t in range(TG):
                nc.vector.bn_stats(out=parts[:, t, :], in_=x_of(gr)[:, t, :])
            for t in range(TG):
                nc.vector.bn_aggr(out=mean_var[:, t, :], in_=parts[:, t, :])
            negmean = stat_pool.tile([P, TG], F32)
            nc.vector.tensor_scalar_mul(out=negmean[:], in0=mean_var[:, :, 0], scalar1=-1.0)
            reciprocal_std(gr, negmean, mean_var[:, :, 1], 1.0)

        def statistics_on_scalar(gr):
            negmean = stat_pool.tile([P, TG], F32)
            sumsq = stat_pool.tile([P, TG], F32)
            junk_a = junk_pool.tile([P, TG, D], BF16)
            junk_b = junk_pool.tile([P, TG, D], BF16)
            for t in range(TG):
                nc.scalar.activation(
                    out=junk_a[:, t, :], in_=x_of(gr)[:, t, :], func=ACT.Copy,
                    scale=-1.0 / D, accum_out=negmean[:, t : t + 1],
                )
            for t in range(TG):
                nc.scalar.activation(
                    out=junk_b[:, t, :], in_=x_of(gr)[:, t, :], func=ACT.Square,
                    bias=negmean[:, t : t + 1], scale=1.0, accum_out=sumsq[:, t : t + 1],
                )
            reciprocal_std(gr, negmean, sumsq[:], 1.0 / D)

        def normalise(gr, help_of_scalar=False):
            negmean, rstd = stats[gr]
            xn = xn_pool.tile([P, TG, PACK, P], F32)
            for t in reversed(range(TG)):
                x_t = x_of(gr)[:, t, :].rearrange("m (p c) -> m c p", c=PACK)
                if help_of_scalar and t == 1:
                    shift = stat_pool.tile([P, 1], F32)
                    nc.gpsimd.tensor_tensor(
                        out=shift[:], in0=negmean[:, t : t + 1], in1=rstd[:, t : t + 1],
                        op=ALU.mult,
                    )
                    nc.scalar.activation(
                        out=xn[:, t, :, :], in_=x_t, func=ACT.Identity,
                        scale=rstd[:, t : t + 1], bias=shift[:, 0:1],
                    )
                else:
                    nc.gpsimd.tensor_scalar(
                        out=xn[:, t, :, :], in0=x_t,
                        scalar1=negmean[:, t : t + 1], scalar2=rstd[:, t : t + 1],
                        op0=ALU.add, op1=ALU.mult,
                    )
            normal[gr] = xn

        def transpose(gr):
            xt = [psum_xt.tile([P, 2, GROUP], F32, name="xt%d" % pair) for pair in range(2)]
            for t in range(TG):
                for c in range(PACK):
                    nc.tensor.transpose(
                        xt[c // 2][:, c % 2, t * P : (t + 1) * P], normal[gr][:, t, c, :], perm[:]
                    )
            banks[gr] = xt

        def gain_and_bias(gr):
            h_planes = h_pool.tile([P, PACK, GROUP], BF16)
            for c in range(PACK):
                nc.scalar.activation(
                    out=h_planes[:, c, :], in_=banks[gr][c // 2][:, c % 2, :], func=ACT.Identity,
                    scale=gb_col[:, c : c + 1], bias=gb_col[:, PACK + c : PACK + c + 1],
                )
            planes[gr] = h_planes

        def regroup(gr, engine):
            h_grouped = h_pool.tile([P, GROUP, PACK], BF16, align_bytes=64)
            engine.tensor_scalar(
                out=h_grouped[:], in0=planes[gr][:].rearrange("p c m -> p m c"),
                scalar1=1.0, scalar2=0.0, op0=ALU.mult, op1=ALU.add,
            )
            grouped[gr] = h_grouped

        def quantise(gr):
            h_codes = q_pool.tile([P, GROUP], U32, align_bytes=64)
            h_scales = q_pool.tile([P, GROUP], U8, align_bytes=64)
            nc.vector.quantize_mx(
                out=h_codes[:].bitcast(FP8X4),
                scales=h_scales[:],
                in_=grouped[gr][:].rearrange("p m c -> p (m c)"),
            )
            codes[gr] = (h_codes, h_scales)

        o_tiles = {}

        def project(u, w, jl):
            cols = slice(w * D, (w + 1) * D)
            if jl == 0:
                o_tiles[u, w] = o_pool.tile([P, HEADS, QUAD, HD], F32, name="o_tile")
            h_codes, h_scales = codes[2 * u + jl // TG]
            tokens = slice((jl % TG) * P, (jl % TG + 1) * P)
            acc = psum_acc.tile([P, D], F32)
            nc.tensor.matmul_mx(
                out=acc[:],
                lhsT=h_codes[:, tokens].bitcast(FP8X4),
                lhsT_scale=h_scales[:, tokens],
                rhs=w_codes[:, cols].bitcast(FP8X4),
                rhs_scale=w_scales[:, cols],
                start=True,
                stop=True,
            )
            nc.vector.tensor_tensor(
                out=o_tiles[u, w][:, :, jl, :],
                in0=acc[:].rearrange("p (h f) -> p h f", h=HEADS),
                in1=bias_bc[:, cols].rearrange("p (h f) -> p h f", h=HEADS),
                op=ALU.add,
            )

        def store(u, w):
            first_window = (u // 2 * 2 + 1 - u % 2) * UNIT_WINDOWS
            nc.sync.dma_start(
                out=outs[w][first_window : first_window + UNIT_WINDOWS].rearrange(
                    "w h (x jl) f -> x (w h) (jl f)", jl=QUAD
                ),
                in_=o_tiles[u, w][:].rearrange("p h jl f -> p h (jl f)"),
            )

        def statistics(gr):
            if gr < 2:
                statistics_on_vector(gr)
            else:
                statistics_on_scalar(gr)

        statistics(0)
        normalise(0, help_of_scalar=True)
        statistics(1)
        widen_gain_and_bias()
        transpose(0)
        normalise(1, help_of_scalar=True)
        regroup_weight(0)
        quantise_weight(0)
        gain_and_bias(0)
        spread_bias(0)
        regroup(0, nc.vector)
        quantise(0)
        transpose(1)
        regroup_weight(1)
        gain_and_bias(1)
        regroup(1, nc.vector)
        quantise(1)
        spread_bias(1)
        statistics(2)
        regroup_weight(2)
        spread_bias(2)
        statistics(3)
        normalise(2)

        for s in range(GROUPS):
            u = s // 2
            turns = [(w, jl) for w in range(3) for jl in range(QUAD)][(s % 2) * 6 : (s % 2) * 6 + 6]
            transpose_at = (5, 2)[s] if s < 2 else 1
            quantise_at = (1, 4)[s % 2]
            if s + 3 < GROUPS:
                normalise(s + 3)
            for n, (w, jl) in enumerate(turns):
                if n == quantise_at and 0 < s < GROUPS - 1:
                    quantise(s + 1)
                if u == 0 and w < 2 and jl == 2:
                    quantise_weight(w + 1)
                project(u, w, jl)
                if n == transpose_at and s + 2 < GROUPS:
                    transpose(s + 2)
                    gain_and_bias(s + 2)
                    regroup(s + 2, nc.gpsimd)
                if jl == QUAD - 1:
                    store(u, w)
            if s + 4 < GROUPS:
                statistics(s + 4)
